import numpy as np
import ml_dtypes


BF16 = ml_dtypes.bfloat16


def bf(x):
    return np.asarray(x, np.float32).astype(BF16)


def f64(x):
    return np.asarray(x).astype(np.float64)


E2M1 = np.array([0.0, 0.5, 1.0, 1.5, 2.0, 3.0, 4.0, 6.0, -0.0, -0.5, -1.0, -1.5, -2.0, -3.0, -4.0, -6.0])


def pack_weight(w, fmt):
    k, n = w.shape
    w = f64(bf(w)).reshape(k // 32, 32, n)
    amax = np.abs(w).max(1)
    if fmt == "e4m3":
        byte = np.frexp(amax)[1] - 1 + 127 - 7
    else:
        mant, ex = np.frexp(amax / 6.0)
        byte = np.where(mant > 0.5, ex, ex - 1) + 127
    byte = np.clip(np.where(amax > 0, byte, 1), 1, 254)
    scaled = (w * np.exp2(127.0 - byte)[:, None, :]).reshape(k, n).astype(np.float32)
    by_word = np.ascontiguousarray(scaled.reshape(k // 512, 128, 4, n).transpose(0, 1, 3, 2))
    if fmt == "e4m3":
        words = by_word.astype(ml_dtypes.float8_e4m3fn).view(np.uint8)
    else:
        c = by_word.astype(ml_dtypes.float4_e2m1fn).view(np.uint8) & 0xF
        words = c[..., 0::2] | (c[..., 1::2] << 4)
    return np.ascontiguousarray(words), np.ascontiguousarray(byte.astype(np.uint8).reshape(k // 512, 16, n))


def unpack_weight(words, scales, fmt):
    g, p, n, _ = words.shape
    if fmt == "e4m3":
        vals = np.ascontiguousarray(words).view(ml_dtypes.float8_e4m3fn).astype(np.float64)
    else:
        nib = np.empty((g, p, n, 4), np.uint8)
        nib[..., 0::2] = words & 0xF
        nib[..., 1::2] = words >> 4
        vals = E2M1[nib]
    vals = vals * np.repeat(np.exp2(scales.astype(np.float64) - 127.0), 8, axis=1)[..., None]
    return vals.transpose(0, 1, 3, 2).reshape(g * 512, n)

def pack4(w):
    words, scales = pack_weight(w, "e2m1")
    return words.reshape(words.shape[0], 128, -1), scales


def unpack4(words, scales):
    return unpack_weight(words.reshape(words.shape[0], 128, -1, 2), scales, "e2m1")


def kspread(k):
    return np.exp2(np.repeat(np.random.randint(-6, 7, k // 32), 32).astype(np.float64))


B, S, H, E, D, TRAIN_LEN = 1, 512, 2048, 2560, 128, 512


def silu(v):
    return v / (1.0 + np.exp(-v))


def apply_rotary(x, sin, cos):
    x1, x2 = x[..., 0::2], x[..., 1::2]
    return np.concatenate([x1 * cos - x2 * sin, x1 * sin + x2 * cos], axis=-1)


def setup_inputs():
    s = kspread(H)
    pos = np.arange(S)[:, None]
    inv = np.exp(-np.arange(0, D, 2) / D * np.log(10000.0))
    ang = pos * inv[None, :]
    hidden_states = np.random.standard_normal((B, S, H)) * s
    hidden_states_words, hidden_states_scales = pack4(np.ascontiguousarray(hidden_states.reshape(B * S, H).T))
    words, scales = pack4(np.random.standard_normal((H, 2 * E + D)) / np.sqrt(H) / s[:, None])
    return {"hidden_states_words": hidden_states_words,
            "hidden_states_scales": hidden_states_scales,
            "sin": bf(np.sin(ang)[None]),
            "cos": bf(np.cos(ang)[None]),
            "W_i_words": words,
            "W_i_scales": scales,
            "q_scale": bf(1.0 + 0.1 * np.random.standard_normal(D)),
            "k_scale": bf(1.0 + 0.1 * np.random.standard_normal(D))}


def reference(hidden_states_words, hidden_states_scales, sin, cos, W_i_words, W_i_scales, q_scale, k_scale):
    x = silu(unpack4(hidden_states_words, hidden_states_scales).T.reshape(B, S, H) @ unpack4(W_i_words, W_i_scales))
    u, v, qk = np.split(x, [E, 2 * E], axis=-1)
    sn, cs = f64(sin), f64(cos)
    q = apply_rotary(qk * f64(q_scale), sn, cs)
    k = apply_rotary(qk * f64(k_scale), sn, cs)
    return u, v, q, k

@@ -1,0 +1,194 @@
+from contextlib import ExitStack
+
+import concourse.mybir as mybir
+
+F32 = mybir.dt.float32
+BF16 = mybir.dt.bfloat16
+I32 = mybir.dt.int32
+U8 = mybir.dt.uint8
+FP4X4 = mybir.dt.float4_e2m1fn_x4
+ADD = mybir.AluOpType.add
+MULT = mybir.AluOpType.mult
+SILU = mybir.ActivationFunctionType.Silu
+
+P = 128
+TOKENS, K, E, D = 512, 2048, 2560, 128
+PASSES = K // 512
+NT = TOKENS // P
+BLOCK = 512
+HALF = D // 2
+FLOPS = 2 * TOKENS * K * (2 * E + D)
+
+
+def tile_gatedattentionunit_pa_kernel(
+    tc, x_words, x_scales, sin, cos, w_words, w_scales, q_scale, k_scale, out_u, out_v, out_q, out_k
+):
+    nc = tc.nc
+    with ExitStack() as ctx:
+        keep = ctx.enter_context(tc.tile_pool(name="keep", bufs=1))
+        results = ctx.enter_context(tc.tile_pool(name="results", bufs=40))
+        work = ctx.enter_context(tc.tile_pool(name="work", bufs=2))
+        psum = ctx.enter_context(tc.psum_pool(name="psum", bufs=8))
+        ctx.enter_context(tc.manual_schedule())
+
+        def words_tile(name, width):
+            return keep.tile([P, PASSES, 2 * width], U8, name=name, align_bytes=256)
+
+        def scale_tile(name, width):
+            return keep.tile([P, PASSES, width], U8, name=name, align_bytes=256)
+
+        def zero(engine, planes):
+            engine.memset(planes[:].rearrange("p g n -> p (g n)").bitcast(I32), 0)
+
+        def load_words(tile, dram, g0, g1, c0, width):
+            nc.sync.dma_start(
+                out=tile[:, g0:g1, :].bitcast(I32),
+                in_=dram[g0:g1, :, 2 * c0 : 2 * (c0 + width)].rearrange("g p n -> p g n").bitcast(I32),
+            )
+
+        def load_scales(planes, dram, c0, width):
+            for q in range(4):
+                nc.sync.dma_start(
+                    out=planes[32 * q : 32 * q + 4, :, :].bitcast(I32),
+                    in_=dram[:, 4 * q : 4 * q + 4, c0 : c0 + width].rearrange("g r n -> r g n").bitcast(I32),
+                )
+
+        xw = words_tile("xw", TOKENS)
+        xs = scale_tile("xs", TOKENS)
+        code_cols = [(0, 512), (512, 512), (1024, 1024), (2048, 512), (4608, 640), (2560, 1024), (3584, 1024)]
+        code_tiles = [words_tile("ww%d" % c0, width) for c0, width in code_cols]
+        plane_cols = [(0, 1024), (1024, 1536), (2560, 2688)]
+        plane_tiles = [scale_tile("ws%d" % c0, width) for c0, width in plane_cols]
+
+        zero(nc.gpsimd, xs)
+        warm = keep.tile([P, BLOCK], BF16, name="warm")
+        nc.vector.memset(warm[:], 0.0)
+        zero(nc.vector, plane_tiles[0])
+
+        warm_acc = psum.tile([P, BLOCK], F32, name="acc")
+        for i in range(12):
+            nc.tensor.matmul(warm_acc[:], lhsT=warm[:, 0:P], rhs=warm[:], start=True, stop=True)
+
+        load_words(xw, x_words, 0, 1, 0, TOKENS)
+        load_words(code_tiles[0], w_words, 0, 1, 0, 512)
+        load_scales(xs, x_scales, 0, TOKENS)
+        load_scales(plane_tiles[0], w_scales, 0, 1024)
+        for g in range(1, PASSES):
+            load_words(xw, x_words, g, g + 1, 0, TOKENS)
+            load_words(code_tiles[0], w_words, g, g + 1, 0, 512)
+        load_words(code_tiles[1], w_words, 0, PASSES, *code_cols[1])
+        zero(nc.vector, plane_tiles[1])
+        zero(nc.vector, plane_tiles[2])
+        load_scales(plane_tiles[1], w_scales, *plane_cols[1])
+        load_words(code_tiles[2], w_words, 0, PASSES, *code_cols[2])
+        load_words(code_tiles[3], w_words, 0, PASSES, *code_cols[3])
+        load_scales(plane_tiles[2], w_scales, *plane_cols[2])
+        for i in range(4, len(code_cols)):
+            load_words(code_tiles[i], w_words, 0, PASSES, *code_cols[i])
+
+        gain_row = keep.tile([P, 2 * D], BF16, name="gain_row")
+        nc.gpsimd.memset(gain_row[:], 0.0)
+        ones = keep.tile([P, P], BF16, name="ones")
+        nc.gpsimd.memset(ones[:], 1.0)
+        nc.gpsimd.dma_start(out=gain_row[0:1, 0:D], in_=q_scale.rearrange("(o n) -> o n", o=1))
+        nc.gpsimd.dma_start(out=gain_row[0:1, D : 2 * D], in_=k_scale.rearrange("(o n) -> o n", o=1))
+        sin_t = keep.tile([P, NT, HALF], BF16, name="sin_t")
+        cos_t = keep.tile([P, NT, HALF], BF16, name="cos_t")
+        nc.gpsimd.dma_start(out=sin_t[:], in_=sin[0].rearrange("(t p) d -> p t d", p=P))
+        nc.gpsimd.dma_start(out=cos_t[:], in_=cos[0].rearrange("(t p) d -> p t d", p=P))
+
+        dummy = keep.tile([P, 1], F32, name="dummy")
+        nc.vector.memset(dummy[:], 0.0)
+        nc.scalar.activation(out=dummy[:], in_=dummy[:], func=SILU)
+
+        def find(cols, c0):
+            for i, (first, width) in enumerate(cols):
+                if first <= c0 < first + width:
+                    return i, c0 - first
+            raise ValueError
+
+        def mm(out, t, g, c0, width):
+            i, a = find(code_cols, c0)
+            j, b = find(plane_cols, c0)
+            nc.tensor.matmul_mx(
+                out=out,
+                lhsT=xw[:, g, 2 * P * t : 2 * P * (t + 1)].bitcast(FP4X4),
+                lhsT_scale=xs[:, g, P * t : P * (t + 1)],
+                rhs=code_tiles[i][:, g, 2 * a : 2 * (a + width)].bitcast(FP4X4),
+                rhs_scale=plane_tiles[j][:, g, b : b + width],
+                start=(g == 0),
+                stop=(g == PASSES - 1),
+            )
+
+        def finish(acc, t, c0, width):
+            result = results.tile([P, BLOCK], F32, name="result")
+            nc.scalar.activation(out=result[:, 0:width], in_=acc[:, 0:width], func=SILU)
+            dst, c = (out_u, c0) if c0 < E else (out_v, c0 - E)
+            nc.sync.dma_start(out=dst[0, P * t : P * (t + 1), c : c + width], in_=result[:, 0:width])
+
+        def tile_block(t, c0, width):
+            acc = psum.tile([P, BLOCK], F32, name="acc")
+            for g in range(PASSES):
+                mm(acc[:, 0:width], t, g, c0, width)
+            finish(acc, t, c0, width)
+
+        accs = []
+        for t in range(NT):
+            acc = psum.tile([P, BLOCK], F32, name="acc")
+            accs.append(acc)
+        for g in range(PASSES):
+            for t in range(NT):
+                mm(accs[t][:], t, g, 0, BLOCK)
+        for t in range(NT):
+            finish(accs[t], t, 0, BLOCK)
+        for t in range(NT):
+            tile_block(t, 512, BLOCK)
+
+        spread = psum.tile([P, BLOCK], F32, name="acc")
+        nc.tensor.matmul(spread[:, 0 : 2 * D], lhsT=ones[:], rhs=gain_row[:], start=True, stop=True)
+        gains = keep.tile([P, 2 * D], F32, name="gains")
+        nc.vector.tensor_copy(out=gains[:], in_=spread[:, 0 : 2 * D])
+        from_even, from_odd = [], []
+        for i in range(2):
+            even = gains[:, D * i : D * (i + 1) : 2].unsqueeze(1).to_broadcast([P, NT, HALF])
+            odd = gains[:, D * i + 1 : D * (i + 1) : 2].unsqueeze(1).to_broadcast([P, NT, HALF])
+            te = keep.tile([P, NT, 2, HALF], F32, name="te%d" % i)
+            to = keep.tile([P, NT, 2, HALF], F32, name="to%d" % i)
+            nc.vector.tensor_tensor(out=te[:, :, 0, :], in0=cos_t[:], in1=even, op=MULT)
+            nc.vector.tensor_tensor(out=te[:, :, 1, :], in0=sin_t[:], in1=even, op=MULT)
+            nc.vector.scalar_tensor_tensor(out=to[:, :, 0, :], in0=sin_t[:], scalar=-1.0, in1=odd, op0=MULT, op1=MULT)
+            nc.vector.tensor_tensor(out=to[:, :, 1, :], in0=cos_t[:], in1=odd, op=MULT)
+            from_even.append(te)
+            from_odd.append(to)
+
+        for c0 in (1024, 1536, 2048):
+            for t in range(NT):
+                tile_block(t, c0, BLOCK)
+
+        qk_acc = psum.tile([P, BLOCK], F32, name="acc")
+        for t in range(NT):
+            for g in range(PASSES):
+                mm(qk_acc[:, D * t : D * (t + 1)], t, g, 2 * E, D)
+        x = keep.tile([P, NT, D], F32, name="x")
+        nc.scalar.activation(out=x[:].rearrange("p t d -> p (t d)"), in_=qk_acc[:], func=SILU)
+        for i, dst in enumerate((out_q, out_k)):
+            x_even = x[:, :, 0:D:2].unsqueeze(2).to_broadcast([P, NT, 2, HALF])
+            x_odd = x[:, :, 1:D:2].unsqueeze(2).to_broadcast([P, NT, 2, HALF])
+            a = work.tile([P, NT, 2, HALF], F32, name="a")
+            b = work.tile([P, NT, 2, HALF], F32, name="b")
+            y = work.tile([P, NT, 2, HALF], F32, name="y")
+            nc.vector.tensor_tensor(out=a[:], in0=from_even[i][:], in1=x_even, op=MULT)
+            nc.vector.tensor_tensor(out=b[:], in0=from_odd[i][:], in1=x_odd, op=MULT)
+            nc.vector.tensor_tensor(out=y[:], in0=a[:], in1=b[:], op=ADD)
+            nc.sync.dma_start(
+                out=dst[0].rearrange("(t p) d -> p t d", p=P), in_=y[:].rearrange("p t h d -> p t (h d)")
+            )
+
+        for c0 in (4608, 2560, 3072, 3584):
+            for t in range(NT):
+                tile_block(t, c0, BLOCK)
+        for t in range(NT - 1):
+            tile_block(t, 4096, BLOCK)
+        tile_block(NT - 1, 4096, 256)
+        tile_block(NT - 1, 4352, 128)
+        tile_block(NT - 1, 4480, 128)

@@ -47,7 +47,7 @@ def tile_gatedattentionunit_pa_kernel(
             )
 
         def load_scales(planes, dram, c0, width):
-            for q in range(4):
+            for q in (0, 2, 1, 3):
                 nc.sync.dma_start(
                     out=planes[32 * q : 32 * q + 4, :, :].bitcast(I32),
                     in_=dram[:, 4 * q : 4 * q + 4, c0 : c0 + width].rearrange("g r n -> r g n").bitcast(I32),
@@ -55,9 +55,9 @@ def tile_gatedattentionunit_pa_kernel(
 
         xw = words_tile("xw", TOKENS)
         xs = scale_tile("xs", TOKENS)
-        code_cols = [(0, 512), (512, 512), (1024, 1024), (2048, 512), (4608, 640), (2560, 1024), (3584, 1024)]
+        code_cols = [(0, 512), (512, 512), (1024, 512), (1536, 512), (2048, 512), (4608, 640), (2560, 1024), (3584, 1024)]
         code_tiles = [words_tile("ww%d" % c0, width) for c0, width in code_cols]
-        plane_cols = [(0, 1024), (1024, 1536), (2560, 2688)]
+        plane_cols = [(0, 512), (512, 1024), (1536, 1024), (2560, 2688)]
         plane_tiles = [scale_tile("ws%d" % c0, width) for c0, width in plane_cols]
 
         zero(nc.gpsimd, xs)
@@ -66,23 +66,21 @@ def tile_gatedattentionunit_pa_kernel(
         zero(nc.vector, plane_tiles[0])
 
         warm_acc = psum.tile([P, BLOCK], F32, name="acc")
-        for i in range(12):
+        for i in range(9):
             nc.tensor.matmul(warm_acc[:], lhsT=warm[:, 0:P], rhs=warm[:], start=True, stop=True)
 
         load_words(xw, x_words, 0, 1, 0, TOKENS)
         load_words(code_tiles[0], w_words, 0, 1, 0, 512)
         load_scales(xs, x_scales, 0, TOKENS)
-        load_scales(plane_tiles[0], w_scales, 0, 1024)
+        load_scales(plane_tiles[0], w_scales, 0, 512)
         for g in range(1, PASSES):
             load_words(xw, x_words, g, g + 1, 0, TOKENS)
             load_words(code_tiles[0], w_words, g, g + 1, 0, 512)
-        load_words(code_tiles[1], w_words, 0, PASSES, *code_cols[1])
-        zero(nc.vector, plane_tiles[1])
-        zero(nc.vector, plane_tiles[2])
-        load_scales(plane_tiles[1], w_scales, *plane_cols[1])
-        load_words(code_tiles[2], w_words, 0, PASSES, *code_cols[2])
-        load_words(code_tiles[3], w_words, 0, PASSES, *code_cols[3])
-        load_scales(plane_tiles[2], w_scales, *plane_cols[2])
+        for planes in plane_tiles[1:]:
+            zero(nc.vector, planes)
+        for j in range(1, 4):
+            load_words(code_tiles[j], w_words, 0, PASSES, *code_cols[j])
+            load_scales(plane_tiles[j], w_scales, *plane_cols[j])
         for i in range(4, len(code_cols)):
             load_words(code_tiles[i], w_words, 0, PASSES, *code_cols[i])
 

@@ -120,7 +120,11 @@ def tile_gatedattentionunit_pa_kernel(
 
         def finish(acc, t, c0, width):
             result = results.tile([P, BLOCK], F32, name="result")
-            nc.scalar.activation(out=result[:, 0:width], in_=acc[:, 0:width], func=SILU)
+            source = acc
+            if t % 2 == 1 and c0 < 4096 and width == BLOCK:
+                source = work.tile([P, BLOCK], F32, name="staged")
+                nc.vector.tensor_copy(out=source[:], in_=acc[:])
+            nc.scalar.activation(out=result[:, 0:width], in_=source[:, 0:width], func=SILU)
             dst, c = (out_u, c0) if c0 < E else (out_v, c0 - E)
             nc.sync.dma_start(out=dst[0, P * t : P * (t + 1), c : c + width], in_=result[:, 0:width])
 

from contextlib import ExitStack

import concourse.mybir as mybir

F32 = mybir.dt.float32
BF16 = mybir.dt.bfloat16
I32 = mybir.dt.int32
U8 = mybir.dt.uint8
FP4X4 = mybir.dt.float4_e2m1fn_x4
ADD = mybir.AluOpType.add
MULT = mybir.AluOpType.mult
SILU = mybir.ActivationFunctionType.Silu

P = 128
TOKENS, K, E, D = 512, 2048, 2560, 128
PASSES = K // 512
NT = TOKENS // P
BLOCK = 512
HALF = D // 2
FLOPS = 2 * TOKENS * K * (2 * E + D)


def tile_gatedattentionunit_pa_kernel(
    tc, x_words, x_scales, sin, cos, w_words, w_scales, q_scale, k_scale, out_u, out_v, out_q, out_k
):
    nc = tc.nc
    with ExitStack() as ctx:
        keep = ctx.enter_context(tc.tile_pool(name="keep", bufs=1))
        results = ctx.enter_context(tc.tile_pool(name="results", bufs=40))
        work = ctx.enter_context(tc.tile_pool(name="work", bufs=2))
        psum = ctx.enter_context(tc.psum_pool(name="psum", bufs=8))
        ctx.enter_context(tc.manual_schedule())

        def words_tile(name, width):
            return keep.tile([P, PASSES, 2 * width], U8, name=name, align_bytes=256)

        def scale_tile(name, width):
            return keep.tile([P, PASSES, width], U8, name=name, align_bytes=256)

        def zero(engine, planes):
            engine.memset(planes[:].rearrange("p g n -> p (g n)").bitcast(I32), 0)

        def load_words(tile, dram, g0, g1, c0, width):
            nc.sync.dma_start(
                out=tile[:, g0:g1, :].bitcast(I32),
                in_=dram[g0:g1, :, 2 * c0 : 2 * (c0 + width)].rearrange("g p n -> p g n").bitcast(I32),
            )

        def load_scales(planes, dram, c0, width):
            for q in (0, 2, 1, 3):
                nc.sync.dma_start(
                    out=planes[32 * q : 32 * q + 4, :, :].bitcast(I32),
                    in_=dram[:, 4 * q : 4 * q + 4, c0 : c0 + width].rearrange("g r n -> r g n").bitcast(I32),
                )

        xw = words_tile("xw", TOKENS)
        xs = scale_tile("xs", TOKENS)
        code_cols = [(0, 512), (512, 512), (1024, 512), (1536, 512), (2048, 512), (4608, 640), (2560, 1024), (3584, 1024)]
        code_tiles = [words_tile("ww%d" % c0, width) for c0, width in code_cols]
        plane_cols = [(0, 512), (512, 1024), (1536, 1024), (2560, 2688)]
        plane_tiles = [scale_tile("ws%d" % c0, width) for c0, width in plane_cols]

        zero(nc.gpsimd, xs)
        warm = keep.tile([P, BLOCK], BF16, name="warm")
        nc.vector.memset(warm[:], 0.0)
        zero(nc.vector, plane_tiles[0])

        warm_acc = psum.tile([P, BLOCK], F32, name="acc")
        for i in range(9):
            nc.tensor.matmul(warm_acc[:], lhsT=warm[:, 0:P], rhs=warm[:], start=True, stop=True)

        load_words(xw, x_words, 0, 1, 0, TOKENS)
        load_words(code_tiles[0], w_words, 0, 1, 0, 512)
        load_scales(xs, x_scales, 0, TOKENS)
        load_scales(plane_tiles[0], w_scales, 0, 512)
        for g in range(1, PASSES):
            load_words(xw, x_words, g, g + 1, 0, TOKENS)
            load_words(code_tiles[0], w_words, g, g + 1, 0, 512)
        for planes in plane_tiles[1:]:
            zero(nc.vector, planes)
        for j in range(1, 4):
            load_words(code_tiles[j], w_words, 0, PASSES, *code_cols[j])
            load_scales(plane_tiles[j], w_scales, *plane_cols[j])
        for i in range(4, len(code_cols)):
            load_words(code_tiles[i], w_words, 0, PASSES, *code_cols[i])

        gain_row = keep.tile([P, 2 * D], BF16, name="gain_row")
        nc.gpsimd.memset(gain_row[:], 0.0)
        ones = keep.tile([P, P], BF16, name="ones")
        nc.gpsimd.memset(ones[:], 1.0)
        nc.gpsimd.dma_start(out=gain_row[0:1, 0:D], in_=q_scale.rearrange("(o n) -> o n", o=1))
        nc.gpsimd.dma_start(out=gain_row[0:1, D : 2 * D], in_=k_scale.rearrange("(o n) -> o n", o=1))
        sin_t = keep.tile([P, NT, HALF], BF16, name="sin_t")
        cos_t = keep.tile([P, NT, HALF], BF16, name="cos_t")
        nc.gpsimd.dma_start(out=sin_t[:], in_=sin[0].rearrange("(t p) d -> p t d", p=P))
        nc.gpsimd.dma_start(out=cos_t[:], in_=cos[0].rearrange("(t p) d -> p t d", p=P))

        dummy = keep.tile([P, 1], F32, name="dummy")
        nc.vector.memset(dummy[:], 0.0)
        nc.scalar.activation(out=dummy[:], in_=dummy[:], func=SILU)

        def find(cols, c0):
            for i, (first, width) in enumerate(cols):
                if first <= c0 < first + width:
                    return i, c0 - first
            raise ValueError

        def mm(out, t, g, c0, width):
            i, a = find(code_cols, c0)
            j, b = find(plane_cols, c0)
            nc.tensor.matmul_mx(
                out=out,
                lhsT=xw[:, g, 2 * P * t : 2 * P * (t + 1)].bitcast(FP4X4),
                lhsT_scale=xs[:, g, P * t : P * (t + 1)],
                rhs=code_tiles[i][:, g, 2 * a : 2 * (a + width)].bitcast(FP4X4),
                rhs_scale=plane_tiles[j][:, g, b : b + width],
                start=(g == 0),
                stop=(g == PASSES - 1),
            )

        def finish(acc, t, c0, width):
            result = results.tile([P, BLOCK], F32, name="result")
            source = acc
            if t % 2 == 1 and c0 < 4096 and width == BLOCK:
                source = work.tile([P, BLOCK], F32, name="staged")
                nc.vector.tensor_copy(out=source[:], in_=acc[:])
            nc.scalar.activation(out=result[:, 0:width], in_=source[:, 0:width], func=SILU)
            dst, c = (out_u, c0) if c0 < E else (out_v, c0 - E)
            nc.sync.dma_start(out=dst[0, P * t : P * (t + 1), c : c + width], in_=result[:, 0:width])

        def tile_block(t, c0, width):
            acc = psum.tile([P, BLOCK], F32, name="acc")
            for g in range(PASSES):
                mm(acc[:, 0:width], t, g, c0, width)
            finish(acc, t, c0, width)

        accs = []
        for t in range(NT):
            acc = psum.tile([P, BLOCK], F32, name="acc")
            accs.append(acc)
        for g in range(PASSES):
            for t in range(NT):
                mm(accs[t][:], t, g, 0, BLOCK)
        for t in range(NT):
            finish(accs[t], t, 0, BLOCK)
        for t in range(NT):
            tile_block(t, 512, BLOCK)

        spread = psum.tile([P, BLOCK], F32, name="acc")
        nc.tensor.matmul(spread[:, 0 : 2 * D], lhsT=ones[:], rhs=gain_row[:], start=True, stop=True)
        gains = keep.tile([P, 2 * D], F32, name="gains")
        nc.vector.tensor_copy(out=gains[:], in_=spread[:, 0 : 2 * D])
        from_even, from_odd = [], []
        for i in range(2):
            even = gains[:, D * i : D * (i + 1) : 2].unsqueeze(1).to_broadcast([P, NT, HALF])
            odd = gains[:, D * i + 1 : D * (i + 1) : 2].unsqueeze(1).to_broadcast([P, NT, HALF])
            te = keep.tile([P, NT, 2, HALF], F32, name="te%d" % i)
            to = keep.tile([P, NT, 2, HALF], F32, name="to%d" % i)
            nc.vector.tensor_tensor(out=te[:, :, 0, :], in0=cos_t[:], in1=even, op=MULT)
            nc.vector.tensor_tensor(out=te[:, :, 1, :], in0=sin_t[:], in1=even, op=MULT)
            nc.vector.scalar_tensor_tensor(out=to[:, :, 0, :], in0=sin_t[:], scalar=-1.0, in1=odd, op0=MULT, op1=MULT)
            nc.vector.tensor_tensor(out=to[:, :, 1, :], in0=cos_t[:], in1=odd, op=MULT)
            from_even.append(te)
            from_odd.append(to)

        for c0 in (1024, 1536, 2048):
            for t in range(NT):
                tile_block(t, c0, BLOCK)

        qk_acc = psum.tile([P, BLOCK], F32, name="acc")
        for t in range(NT):
            for g in range(PASSES):
                mm(qk_acc[:, D * t : D * (t + 1)], t, g, 2 * E, D)
        x = keep.tile([P, NT, D], F32, name="x")
        nc.scalar.activation(out=x[:].rearrange("p t d -> p (t d)"), in_=qk_acc[:], func=SILU)
        for i, dst in enumerate((out_q, out_k)):
            x_even = x[:, :, 0:D:2].unsqueeze(2).to_broadcast([P, NT, 2, HALF])
            x_odd = x[:, :, 1:D:2].unsqueeze(2).to_broadcast([P, NT, 2, HALF])
            a = work.tile([P, NT, 2, HALF], F32, name="a")
            b = work.tile([P, NT, 2, HALF], F32, name="b")
            y = work.tile([P, NT, 2, HALF], F32, name="y")
            nc.vector.tensor_tensor(out=a[:], in0=from_even[i][:], in1=x_even, op=MULT)
            nc.vector.tensor_tensor(out=b[:], in0=from_odd[i][:], in1=x_odd, op=MULT)
            nc.vector.tensor_tensor(out=y[:], in0=a[:], in1=b[:], op=ADD)
            nc.sync.dma_start(
                out=dst[0].rearrange("(t p) d -> p t d", p=P), in_=y[:].rearrange("p t h d -> p t (h d)")
            )

        for c0 in (4608, 2560, 3072, 3584):
            for t in range(NT):
                tile_block(t, c0, BLOCK)
        for t in range(NT - 1):
            tile_block(t, 4096, BLOCK)
        tile_block(NT - 1, 4096, 256)
        tile_block(NT - 1, 4352, 128)
        tile_block(NT - 1, 4480, 128)
